import numpy as np
import ml_dtypes


def mxq(x, axis, fmt="e4m3"):
    dtype, down = {"e4m3": (ml_dtypes.float8_e4m3fn, 7), "e5m2": (ml_dtypes.float8_e5m2, 14)}[fmt]
    v = np.moveaxis(np.asarray(x, np.float32).astype(ml_dtypes.bfloat16).astype(np.float64), axis, -1)
    blocks = v.reshape(v.shape[:-1] + (-1, 32))
    amax = np.abs(blocks).max(-1, keepdims=True)
    byte = np.maximum(np.where(amax > 0, np.frexp(amax)[1] - 1 + 127, 0) - down, 1)
    scale = np.exp2(byte - 127.0)
    codes = (blocks / scale).astype(np.float32).astype(dtype).astype(np.float64)
    return np.moveaxis((codes * scale).reshape(v.shape), -1, axis)


WIDE = False


def mx_kscale(k):
    if not WIDE:
        return np.ones(k)
    levels = np.array([10, -10, 5, -5, 0])
    a = np.random.permutation(np.resize(levels, k // 512 * 4)).reshape(k // 512, 4)
    idx = np.arange(k)
    return np.exp2(a[idx // 512, idx % 128 // 32])


BF16 = ml_dtypes.bfloat16


def bf(x):
    return np.asarray(x, np.float32).astype(BF16)


def f64(x):
    return np.asarray(x).astype(np.float64)


E2M1 = np.array([0.0, 0.5, 1.0, 1.5, 2.0, 3.0, 4.0, 6.0, -0.0, -0.5, -1.0, -1.5, -2.0, -3.0, -4.0, -6.0])


def pack_weight(w, fmt):
    k, n = w.shape
    w = f64(bf(w)).reshape(k // 32, 32, n)
    amax = np.abs(w).max(1)
    if fmt == "e4m3":
        byte = np.frexp(amax)[1] - 1 + 127 - 7
    else:
        mant, ex = np.frexp(amax / 6.0)
        byte = np.where(mant > 0.5, ex, ex - 1) + 127
    byte = np.clip(np.where(amax > 0, byte, 1), 1, 254)
    scaled = (w * np.exp2(127.0 - byte)[:, None, :]).reshape(k, n).astype(np.float32)
    by_word = np.ascontiguousarray(scaled.reshape(k // 512, 128, 4, n).transpose(0, 1, 3, 2))
    if fmt == "e4m3":
        words = by_word.astype(ml_dtypes.float8_e4m3fn).view(np.uint8)
    else:
        c = by_word.astype(ml_dtypes.float4_e2m1fn).view(np.uint8) & 0xF
        words = c[..., 0::2] | (c[..., 1::2] << 4)
    return np.ascontiguousarray(words), np.ascontiguousarray(byte.astype(np.uint8).reshape(k // 512, 16, n))


def unpack_weight(words, scales, fmt):
    g, p, n, _ = words.shape
    if fmt == "e4m3":
        vals = np.ascontiguousarray(words).view(ml_dtypes.float8_e4m3fn).astype(np.float64)
    else:
        nib = np.empty((g, p, n, 4), np.uint8)
        nib[..., 0::2] = words & 0xF
        nib[..., 1::2] = words >> 4
        vals = E2M1[nib]
    vals = vals * np.repeat(np.exp2(scales.astype(np.float64) - 127.0), 8, axis=1)[..., None]
    return vals.transpose(0, 1, 3, 2).reshape(g * 512, n)


B, N, C, D = 2, 128, 16384, 512
ETA, TAU = 1.0, 1.5
FMT = "e4m3"


def setup_inputs():
    s, t = mx_kscale(C), mx_kscale(D)
    a = 2.0 * (C / D) ** 0.25 / np.sqrt(C)
    H_t = bf(np.random.standard_normal((B, N, C)) * s)
    A_stat = bf(np.random.random((N, N)))
    M_mask = bf(np.random.random((N, N)) - 0.25)
    Wq = np.random.standard_normal((D, C)) * a * t[:, None] / s
    Wk = np.random.standard_normal((D, C)) * a / t[:, None] / s
    Wq_words, Wq_scales = pack_weight(np.ascontiguousarray(Wq.T), FMT)
    Wk_words, Wk_scales = pack_weight(np.ascontiguousarray(Wk.T), FMT)
    return {"H_t": H_t,
            "A_stat": A_stat,
            "M_mask": M_mask,
            "Wq_words": Wq_words,
            "Wq_scales": Wq_scales,
            "Wk_words": Wk_words,
            "Wk_scales": Wk_scales}


def reference(H_t, A_stat, M_mask, Wq_words, Wq_scales, Wk_words, Wk_scales):
    c = H_t.shape[-1]
    hq = mxq(f64(H_t), 2, "e4m3")
    Q = hq @ unpack_weight(Wq_words, Wq_scales, FMT)
    K = hq @ unpack_weight(Wk_words, Wk_scales, FMT)
    logits = (mxq(Q, 2, "e4m3") @ mxq(K, 2, "e4m3").transpose(0, 2, 1)) / (np.sqrt(c) * TAU)
    logits = 0.5 * (logits + logits.transpose(0, 2, 1))
    n = logits.shape[-1]
    eye = np.eye(n, dtype=bool)
    logits = np.where(eye[None, :, :], -np.inf, logits)
    A_bias = np.where(eye, 0.0, f64(A_stat))
    logits = logits + ETA * A_bias[None, :, :]
    logits = np.where((f64(M_mask) <= 0)[None, :, :], -np.inf, logits)
    e = np.exp(logits - logits.max(-1, keepdims=True))
    return e / e.sum(-1, keepdims=True)

@@ -1,0 +1,232 @@
+import math
+from contextlib import ExitStack
+
+import concourse.mybir as mybir
+from concourse.masks import make_identity
+
+F32 = mybir.dt.float32
+BF16 = mybir.dt.bfloat16
+I32 = mybir.dt.int32
+U32 = mybir.dt.uint32
+U8 = mybir.dt.uint8
+FP8X4 = mybir.dt.float8_e4m3fn_x4
+ALU = mybir.AluOpType
+ACT = mybir.ActivationFunctionType
+
+P = 128
+PACK = 4
+K_PASS = P * PACK
+B = 2
+NODES = 128
+TOKENS = B * NODES
+C = 16384
+D = 512
+TAU = 1.5
+PASSES = C // K_PASS
+D_BLOCKS = D // P
+RUN = 4
+CHUNKS = PASSES // RUN
+QUADRANTS = 4
+LIVE = 4
+AHEAD = 4
+W_BUFS = 12
+EXCLUDED = -1.0e30
+SCORE_SCALE = 0.5 / (math.sqrt(C) * TAU)
+
+FLOPS = 2 * TOKENS * C * 2 * D + 2 * B * NODES * NODES * D
+
+
+def tile_dynamicgraphattention_k_kernel(
+    tc, H_t, A_stat, M_mask, Wq_words, Wq_scales, Wk_words, Wk_scales, out
+):
+    nc = tc.nc
+    with ExitStack() as ctx:
+        keep = ctx.enter_context(tc.tile_pool(name="keep", bufs=1))
+        h_pool = ctx.enter_context(tc.tile_pool(name="h_pool", bufs=AHEAD))
+        g_pool = ctx.enter_context(tc.tile_pool(name="g_pool", bufs=2))
+        w_pool = ctx.enter_context(tc.tile_pool(name="w_pool", bufs=W_BUFS))
+        psum = ctx.enter_context(tc.psum_pool(name="psum", bufs=1))
+        ctx.enter_context(tc.manual_schedule())
+
+        h_words = keep.tile([P, PASSES * TOKENS], U32, align_bytes=64)
+        h_planes = keep.tile([P, PASSES * TOKENS], U8, align_bytes=64)
+        planes = {
+            "q": keep.tile([P, CHUNKS, D], U8, name="q_planes", align_bytes=64),
+            "k": keep.tile([P, CHUNKS, D], U8, name="k_planes", align_bytes=64),
+        }
+        words_in = {"q": Wq_words, "k": Wk_words}
+        scales_in = {"q": Wq_scales, "k": Wk_scales}
+        w_order = [("q", c) for c in range(CHUNKS)] + [("k", c) for c in range(CHUNKS)]
+        w_tiles = {}
+        h_tiles = {}
+
+        def load_h(c):
+            h_raw = h_pool.tile([P, B, RUN * K_PASS], BF16)
+            cols = slice(c * RUN * K_PASS, (c + 1) * RUN * K_PASS)
+            nc.sync.dma_start(out=h_raw[:], in_=H_t.rearrange("b n c -> n b c")[:, :, cols])
+            h_tiles[c] = h_raw
+
+        def load_w(which, c):
+            group = slice(c * RUN, (c + 1) * RUN)
+            for quad in range(QUADRANTS):
+                nc.sync.dma_start(
+                    out=planes[which][32 * quad : 32 * quad + RUN * LIVE, c, :].bitcast(I32),
+                    in_=scales_in[which][group, LIVE * quad : LIVE * (quad + 1), :].bitcast(I32),
+                )
+            w_words = w_pool.tile([P, RUN, D], U32, align_bytes=64)
+            by_partition = words_in[which].rearrange("g p n t -> p g (n t)")
+            nc.sync.dma_start(out=w_words[:].bitcast(I32), in_=by_partition[:, group, :].bitcast(I32))
+            w_tiles[(which, c)] = w_words
+
+        for which in ("q", "k"):
+            nc.vector.memset(planes[which][:].bitcast(I32), 0)
+        ident = keep.tile([P, P], F32)
+        make_identity(nc, ident[:])
+        a_stat = keep.tile([P, NODES], BF16)
+        m_mask = keep.tile([P, NODES], BF16)
+        nc.scalar.dma_start(out=a_stat[:], in_=A_stat)
+        nc.scalar.dma_start(out=m_mask[:], in_=M_mask)
+        for c in range(AHEAD):
+            load_h(c)
+            load_w(*w_order[c])
+
+        zero = keep.tile([P, 1], F32)
+        one = keep.tile([P, 1], F32)
+        nc.vector.memset(zero[:], 0.0)
+        nc.scalar.activation(out=one[:], in_=zero[:], func=ACT.Exp)
+
+        excluded = keep.tile([P, NODES], F32)
+        bias = keep.tile([P, NODES], F32)
+        nc.vector.tensor_scalar(out=excluded[:], in0=m_mask[:], scalar1=0.0, scalar2=None, op0=ALU.is_le)
+        nc.vector.tensor_tensor(out=excluded[:], in0=excluded[:], in1=ident[:], op=ALU.max)
+        nc.vector.scalar_tensor_tensor(
+            out=bias[:], in0=excluded[:], scalar=EXCLUDED, in1=a_stat[:], op0=ALU.mult, op1=ALU.add
+        )
+
+        def out_of_psum(index, out_ap, in_ap):
+            if index % 2 == 0:
+                nc.scalar.copy(out=out_ap, in_=in_ap)
+            else:
+                nc.vector.tensor_copy(out=out_ap, in_=in_ap)
+
+        def transpose_chunk(c):
+            pairs = h_tiles[c][:].bitcast(F32)
+            grouped = g_pool.tile([P, RUN, TOKENS, PACK], BF16, align_bytes=64)
+            grouped_pairs = grouped[:].bitcast(F32)
+            for i in range(RUN):
+                flipped = psum.tile([P, 2, TOKENS], F32, name="flip%d" % i)
+                for u in range(2):
+                    for b in range(B):
+                        nc.tensor.transpose(
+                            flipped[:, u, b * NODES : (b + 1) * NODES],
+                            pairs[:, b, 256 * i + u : 256 * (i + 1) : 2],
+                            ident[:],
+                        )
+                out_of_psum(i, grouped_pairs[:, i], flipped[:].rearrange("p u r -> p r u"))
+            return grouped
+
+        def quantise_chunk(c, grouped):
+            cols = slice(c * RUN * TOKENS, (c + 1) * RUN * TOKENS)
+            nc.vector.quantize_mx(
+                out=h_words[:, cols].bitcast(FP8X4),
+                scales=h_planes[:, cols],
+                in_=grouped[:].rearrange("p i r t -> p (i r t)"),
+            )
+
+        def project_chunk(which, c, acc):
+            w_words = w_tiles[(which, c)]
+            for i in range(RUN):
+                g = c * RUN + i
+                tokens = slice(g * TOKENS, (g + 1) * TOKENS)
+                for j in range(D_BLOCKS):
+                    features = slice(j * P, (j + 1) * P)
+                    nc.tensor.matmul_mx(
+                        out=acc[j][:],
+                        lhsT=w_words[:, i, features].bitcast(FP8X4),
+                        lhsT_scale=planes[which][LIVE * i : P, c, features],
+                        rhs=h_words[:, tokens].bitcast(FP8X4),
+                        rhs_scale=h_planes[:, tokens],
+                        start=(g == 0),
+                        stop=(g == PASSES - 1),
+                    )
+
+        def quantise_projection(which, acc):
+            rounded = keep.tile([P, D_BLOCKS, TOKENS], BF16, name=which + "_rounded")
+            for j in range(D_BLOCKS):
+                out_of_psum(j, rounded[:, j, :], acc[j][:])
+            grouped = keep.tile([P, TOKENS, PACK], BF16, name=which + "_grouped", align_bytes=64)
+            nc.vector.tensor_copy(out=grouped[:], in_=rounded[:].rearrange("p t r -> p r t"))
+            codes = keep.tile([P, TOKENS], U32, name=which + "_codes", align_bytes=64)
+            plane = keep.tile([P, TOKENS], U8, name=which + "_plane", align_bytes=64)
+            nc.vector.quantize_mx(
+                out=codes[:].bitcast(FP8X4),
+                scales=plane[:],
+                in_=grouped[:].rearrange("p r t -> p (r t)"),
+            )
+            return codes, plane
+
+        def load_ahead(step):
+            if step + AHEAD < CHUNKS:
+                load_h(step + AHEAD)
+            if step + AHEAD < len(w_order):
+                load_w(*w_order[step + AHEAD])
+
+        q_acc = [psum.tile([P, TOKENS], F32, name="q_acc%d" % j) for j in range(D_BLOCKS)]
+        for c in range(CHUNKS):
+            grouped = transpose_chunk(c)
+            load_ahead(c)
+            quantise_chunk(c, grouped)
+            if c > 0:
+                project_chunk("q", c - 1, q_acc)
+        project_chunk("q", CHUNKS - 1, q_acc)
+        q_codes, q_plane = quantise_projection("q", q_acc)
+
+        k_acc = [
+            psum.tile([P, TOKENS], F32, name="k_acc%d" % j, tag="flip%d" % j) for j in range(D_BLOCKS)
+        ]
+        for c in range(CHUNKS):
+            load_ahead(CHUNKS + c)
+            project_chunk("k", c, k_acc)
+        k_codes, k_plane = quantise_projection("k", k_acc)
+
+        logits = psum.tile([P, B, NODES], F32, tag="q_acc0")
+        for b in range(B):
+            nodes = slice(b * NODES, (b + 1) * NODES)
+            sides = ((q_codes, q_plane, k_codes, k_plane), (k_codes, k_plane, q_codes, q_plane))
+            for turn, (l_codes, l_plane, r_codes, r_plane) in enumerate(sides):
+                nc.tensor.matmul_mx(
+                    out=logits[:, b, :],
+                    lhsT=l_codes[:, nodes].bitcast(FP8X4),
+                    lhsT_scale=l_plane[:, nodes],
+                    rhs=r_codes[:, nodes].bitcast(FP8X4),
+                    rhs_scale=r_plane[:, nodes],
+                    start=(turn == 0),
+                    stop=(turn == 1),
+                )
+        scores = keep.tile([P, B, NODES], F32)
+        neg_max = keep.tile([P, B], F32)
+        weights = keep.tile([P, B, NODES], F32)
+        sums = keep.tile([P, B], F32)
+        inverse = keep.tile([P, B], F32)
+        result = keep.tile([P, B, NODES], F32)
+        for b in range(B):
+            nc.vector.scalar_tensor_tensor(
+                out=scores[:, b, :], in0=logits[:, b, :], scalar=SCORE_SCALE, in1=bias[:],
+                op0=ALU.mult, op1=ALU.add,
+            )
+        for b in range(B):
+            nc.vector.tensor_reduce(
+                out=neg_max[:, b : b + 1], in_=scores[:, b, :], axis=mybir.AxisListType.X,
+                op=ALU.max, negate=True,
+            )
+            nc.scalar.activation(
+                out=weights[:, b, :], in_=scores[:, b, :], func=ACT.Exp,
+                bias=neg_max[:, b : b + 1], scale=1.0, accum_out=sums[:, b : b + 1],
+            )
+        for b in range(B):
+            nc.vector.reciprocal(out=inverse[:, b : b + 1], in_=sums[:, b : b + 1])
+            nc.vector.tensor_scalar(
+                out=result[:, b, :], in0=weights[:, b, :], scalar1=inverse[:, b : b + 1],
+                scalar2=None, op0=ALU.mult,
+            )
+        nc.sync.dma_start(out=out.rearrange("b n m -> n b m"), in_=result[:])

@@ -75,7 +75,13 @@ def tile_dynamicgraphattention_k_kernel(
                 )
             w_words = w_pool.tile([P, RUN, D], U32, align_bytes=64)
             by_partition = words_in[which].rearrange("g p n t -> p g (n t)")
-            nc.sync.dma_start(out=w_words[:].bitcast(I32), in_=by_partition[:, group, :].bitcast(I32))
+            if (which, c) == w_order[-1]:
+                for i in range(RUN):
+                    nc.sync.dma_start(
+                        out=w_words[:, i, :].bitcast(I32), in_=by_partition[:, c * RUN + i, :].bitcast(I32)
+                    )
+            else:
+                nc.sync.dma_start(out=w_words[:].bitcast(I32), in_=by_partition[:, group, :].bitcast(I32))
             w_tiles[(which, c)] = w_words
 
         for which in ("q", "k"):

@@ -28,7 +28,8 @@ RUN = 4
 CHUNKS = PASSES // RUN
 QUADRANTS = 4
 LIVE = 4
-AHEAD = 4
+H_BUFS = 4
+LEAD = 2
 W_BUFS = 12
 EXCLUDED = -1.0e30
 SCORE_SCALE = 0.5 / (math.sqrt(C) * TAU)
@@ -42,7 +43,7 @@ def tile_dynamicgraphattention_k_kernel(
     nc = tc.nc
     with ExitStack() as ctx:
         keep = ctx.enter_context(tc.tile_pool(name="keep", bufs=1))
-        h_pool = ctx.enter_context(tc.tile_pool(name="h_pool", bufs=AHEAD))
+        h_pool = ctx.enter_context(tc.tile_pool(name="h_pool", bufs=H_BUFS))
         g_pool = ctx.enter_context(tc.tile_pool(name="g_pool", bufs=2))
         w_pool = ctx.enter_context(tc.tile_pool(name="w_pool", bufs=W_BUFS))
         psum = ctx.enter_context(tc.psum_pool(name="psum", bufs=1))
@@ -84,30 +85,26 @@ def tile_dynamicgraphattention_k_kernel(
                 nc.sync.dma_start(out=w_words[:].bitcast(I32), in_=by_partition[:, group, :].bitcast(I32))
             w_tiles[(which, c)] = w_words
 
+        def load_stream(n):
+            if n + LEAD - 1 < CHUNKS:
+                load_h(n + LEAD - 1)
+            if n < len(w_order):
+                load_w(*w_order[n])
+
         for which in ("q", "k"):
             nc.vector.memset(planes[which][:].bitcast(I32), 0)
         ident = keep.tile([P, P], F32)
         make_identity(nc, ident[:])
-        a_stat = keep.tile([P, NODES], BF16)
-        m_mask = keep.tile([P, NODES], BF16)
-        nc.scalar.dma_start(out=a_stat[:], in_=A_stat)
-        nc.scalar.dma_start(out=m_mask[:], in_=M_mask)
-        for c in range(AHEAD):
+        for c in range(LEAD):
             load_h(c)
-            load_w(*w_order[c])
+        load_w(*w_order[0])
+        for n in range(1, H_BUFS - LEAD + 1):
+            load_stream(n)
 
         zero = keep.tile([P, 1], F32)
         one = keep.tile([P, 1], F32)
         nc.vector.memset(zero[:], 0.0)
         nc.scalar.activation(out=one[:], in_=zero[:], func=ACT.Exp)
-
-        excluded = keep.tile([P, NODES], F32)
-        bias = keep.tile([P, NODES], F32)
-        nc.vector.tensor_scalar(out=excluded[:], in0=m_mask[:], scalar1=0.0, scalar2=None, op0=ALU.is_le)
-        nc.vector.tensor_tensor(out=excluded[:], in0=excluded[:], in1=ident[:], op=ALU.max)
-        nc.vector.scalar_tensor_tensor(
-            out=bias[:], in0=excluded[:], scalar=EXCLUDED, in1=a_stat[:], op0=ALU.mult, op1=ALU.add
-        )
 
         def out_of_psum(index, out_ap, in_ap):
             if index % 2 == 0:
@@ -156,44 +153,68 @@ def tile_dynamicgraphattention_k_kernel(
                         stop=(g == PASSES - 1),
                     )
 
-        def quantise_projection(which, acc):
+        def quantise_projection(which, acc, between=(None, None, None)):
             rounded = keep.tile([P, D_BLOCKS, TOKENS], BF16, name=which + "_rounded")
             for j in range(D_BLOCKS):
                 out_of_psum(j, rounded[:, j, :], acc[j][:])
             grouped = keep.tile([P, TOKENS, PACK], BF16, name=which + "_grouped", align_bytes=64)
-            nc.vector.tensor_copy(out=grouped[:], in_=rounded[:].rearrange("p t r -> p r t"))
             codes = keep.tile([P, TOKENS], U32, name=which + "_codes", align_bytes=64)
             plane = keep.tile([P, TOKENS], U8, name=which + "_plane", align_bytes=64)
-            nc.vector.quantize_mx(
-                out=codes[:].bitcast(FP8X4),
-                scales=plane[:],
-                in_=grouped[:].rearrange("p r t -> p (r t)"),
+            halves = [slice(b * NODES, (b + 1) * NODES) for b in range(B)]
+            nc.vector.tensor_copy(
+                out=grouped[:, halves[0], :], in_=rounded[:, :, halves[0]].rearrange("p t r -> p r t")
             )
+            nc.scalar.copy(
+                out=grouped[:, halves[1], :], in_=rounded[:, :, halves[1]].rearrange("p t r -> p r t")
+            )
+            for b, nodes in enumerate(halves):
+                if between[b] is not None:
+                    between[b]()
+                nc.vector.quantize_mx(
+                    out=codes[:, nodes].bitcast(FP8X4),
+                    scales=plane[:, nodes],
+                    in_=grouped[:, nodes, :].rearrange("p r t -> p (r t)"),
+                )
+            if between[B] is not None:
+                between[B]()
             return codes, plane
 
-        def load_ahead(step):
-            if step + AHEAD < CHUNKS:
-                load_h(step + AHEAD)
-            if step + AHEAD < len(w_order):
-                load_w(*w_order[step + AHEAD])
 
         q_acc = [psum.tile([P, TOKENS], F32, name="q_acc%d" % j) for j in range(D_BLOCKS)]
-        for c in range(CHUNKS):
-            grouped = transpose_chunk(c)
-            load_ahead(c)
-            quantise_chunk(c, grouped)
-            if c > 0:
-                project_chunk("q", c - 1, q_acc)
-        project_chunk("q", CHUNKS - 1, q_acc)
+        for c in range(-LEAD, CHUNKS):
+            if c >= 0:
+                project_chunk("q", c, q_acc)
+            if c + LEAD < CHUNKS:
+                grouped = transpose_chunk(c + LEAD)
+            load_stream(c + H_BUFS + 1)
+            if c + LEAD < CHUNKS:
+                quantise_chunk(c + LEAD, grouped)
         q_codes, q_plane = quantise_projection("q", q_acc)
 
         k_acc = [
             psum.tile([P, TOKENS], F32, name="k_acc%d" % j, tag="flip%d" % j) for j in range(D_BLOCKS)
         ]
         for c in range(CHUNKS):
-            load_ahead(CHUNKS + c)
+            load_stream(CHUNKS + H_BUFS + 1 + c)
             project_chunk("k", c, k_acc)
-        k_codes, k_plane = quantise_projection("k", k_acc)
+        a_stat = keep.tile([P, NODES], BF16)
+        m_mask = keep.tile([P, NODES], BF16)
+        nc.sync.dma_start(out=a_stat[:], in_=A_stat)
+        nc.sync.dma_start(out=m_mask[:], in_=M_mask)
+        masked = keep.tile([P, NODES], F32)
+        excluded = keep.tile([P, NODES], F32)
+        bias = keep.tile([P, NODES], F32)
+        bias_steps = (
+            lambda: nc.vector.tensor_scalar(
+                out=masked[:], in0=m_mask[:], scalar1=0.0, scalar2=None, op0=ALU.is_le
+            ),
+            lambda: nc.vector.tensor_tensor(out=excluded[:], in0=masked[:], in1=ident[:], op=ALU.max),
+            lambda: nc.vector.scalar_tensor_tensor(
+                out=bias[:], in0=excluded[:], scalar=EXCLUDED, in1=a_stat[:], op0=ALU.mult, op1=ALU.add
+            ),
+        )
+        k_codes, k_plane = quantise_projection("k", k_acc, between=bias_steps)
+
 
         logits = psum.tile([P, B, NODES], F32, tag="q_acc0")
         for b in range(B):

@@ -67,13 +67,20 @@ def tile_dynamicgraphattention_k_kernel(
             nc.sync.dma_start(out=h_raw[:], in_=H_t.rearrange("b n c -> n b c")[:, :, cols])
             h_tiles[c] = h_raw
 
-        def load_w(which, c):
+        def load_scales(which, c):
             group = slice(c * RUN, (c + 1) * RUN)
             for quad in range(QUADRANTS):
-                nc.sync.dma_start(
-                    out=planes[which][32 * quad : 32 * quad + RUN * LIVE, c, :].bitcast(I32),
-                    in_=scales_in[which][group, LIVE * quad : LIVE * (quad + 1), :].bitcast(I32),
-                )
+                rows_out = planes[which][32 * quad : 32 * quad + RUN * LIVE, c, :]
+                rows_in = scales_in[which][group, LIVE * quad : LIVE * (quad + 1), :]
+                if which == "q":
+                    nc.sync.dma_start(out=rows_out.bitcast(I32), in_=rows_in.bitcast(I32))
+                else:
+                    nc.gpsimd.dma_start(out=rows_out.bitcast(F32), in_=rows_in.bitcast(F32))
+
+        def load_w(which, c):
+            group = slice(c * RUN, (c + 1) * RUN)
+            if which == "q":
+                load_scales(which, c)
             w_words = w_pool.tile([P, RUN, D], U32, align_bytes=64)
             by_partition = words_in[which].rearrange("g p n t -> p g (n t)")
             if (which, c) == w_order[-1]:
@@ -95,6 +102,8 @@ def tile_dynamicgraphattention_k_kernel(
             nc.vector.memset(planes[which][:].bitcast(I32), 0)
         ident = keep.tile([P, P], F32)
         make_identity(nc, ident[:])
+        for c in range(CHUNKS):
+            load_scales("k", c)
         for c in range(LEAD):
             load_h(c)
         load_w(*w_order[0])

@@ -72,14 +72,14 @@ def tile_dynamicgraphattention_k_kernel(
             for quad in range(QUADRANTS):
                 rows_out = planes[which][32 * quad : 32 * quad + RUN * LIVE, c, :]
                 rows_in = scales_in[which][group, LIVE * quad : LIVE * (quad + 1), :]
-                if which == "q":
+                if which == "k":
                     nc.sync.dma_start(out=rows_out.bitcast(I32), in_=rows_in.bitcast(I32))
                 else:
                     nc.gpsimd.dma_start(out=rows_out.bitcast(F32), in_=rows_in.bitcast(F32))
 
         def load_w(which, c):
             group = slice(c * RUN, (c + 1) * RUN)
-            if which == "q":
+            if which == "k":
                 load_scales(which, c)
             w_words = w_pool.tile([P, RUN, D], U32, align_bytes=64)
             by_partition = words_in[which].rearrange("g p n t -> p g (n t)")
@@ -103,7 +103,7 @@ def tile_dynamicgraphattention_k_kernel(
         ident = keep.tile([P, P], F32)
         make_identity(nc, ident[:])
         for c in range(CHUNKS):
-            load_scales("k", c)
+            load_scales("q", c)
         for c in range(LEAD):
             load_h(c)
         load_w(*w_order[0])

import math
from contextlib import ExitStack

import concourse.mybir as mybir
from concourse.masks import make_identity

F32 = mybir.dt.float32
BF16 = mybir.dt.bfloat16
I32 = mybir.dt.int32
U32 = mybir.dt.uint32
U8 = mybir.dt.uint8
FP8X4 = mybir.dt.float8_e4m3fn_x4
ALU = mybir.AluOpType
ACT = mybir.ActivationFunctionType

P = 128
PACK = 4
K_PASS = P * PACK
B = 2
NODES = 128
TOKENS = B * NODES
C = 16384
D = 512
TAU = 1.5
PASSES = C // K_PASS
D_BLOCKS = D // P
RUN = 4
CHUNKS = PASSES // RUN
QUADRANTS = 4
LIVE = 4
H_BUFS = 4
LEAD = 2
W_BUFS = 12
EXCLUDED = -1.0e30
SCORE_SCALE = 0.5 / (math.sqrt(C) * TAU)

FLOPS = 2 * TOKENS * C * 2 * D + 2 * B * NODES * NODES * D


def tile_dynamicgraphattention_k_kernel(
    tc, H_t, A_stat, M_mask, Wq_words, Wq_scales, Wk_words, Wk_scales, out
):
    nc = tc.nc
    with ExitStack() as ctx:
        keep = ctx.enter_context(tc.tile_pool(name="keep", bufs=1))
        h_pool = ctx.enter_context(tc.tile_pool(name="h_pool", bufs=H_BUFS))
        g_pool = ctx.enter_context(tc.tile_pool(name="g_pool", bufs=2))
        w_pool = ctx.enter_context(tc.tile_pool(name="w_pool", bufs=W_BUFS))
        psum = ctx.enter_context(tc.psum_pool(name="psum", bufs=1))
        ctx.enter_context(tc.manual_schedule())

        h_words = keep.tile([P, PASSES * TOKENS], U32, align_bytes=64)
        h_planes = keep.tile([P, PASSES * TOKENS], U8, align_bytes=64)
        planes = {
            "q": keep.tile([P, CHUNKS, D], U8, name="q_planes", align_bytes=64),
            "k": keep.tile([P, CHUNKS, D], U8, name="k_planes", align_bytes=64),
        }
        words_in = {"q": Wq_words, "k": Wk_words}
        scales_in = {"q": Wq_scales, "k": Wk_scales}
        w_order = [("q", c) for c in range(CHUNKS)] + [("k", c) for c in range(CHUNKS)]
        w_tiles = {}
        h_tiles = {}

        def load_h(c):
            h_raw = h_pool.tile([P, B, RUN * K_PASS], BF16)
            cols = slice(c * RUN * K_PASS, (c + 1) * RUN * K_PASS)
            nc.sync.dma_start(out=h_raw[:], in_=H_t.rearrange("b n c -> n b c")[:, :, cols])
            h_tiles[c] = h_raw

        def load_scales(which, c):
            group = slice(c * RUN, (c + 1) * RUN)
            for quad in range(QUADRANTS):
                rows_out = planes[which][32 * quad : 32 * quad + RUN * LIVE, c, :]
                rows_in = scales_in[which][group, LIVE * quad : LIVE * (quad + 1), :]
                if which == "k":
                    nc.sync.dma_start(out=rows_out.bitcast(I32), in_=rows_in.bitcast(I32))
                else:
                    nc.gpsimd.dma_start(out=rows_out.bitcast(F32), in_=rows_in.bitcast(F32))

        def load_w(which, c):
            group = slice(c * RUN, (c + 1) * RUN)
            if which == "k":
                load_scales(which, c)
            w_words = w_pool.tile([P, RUN, D], U32, align_bytes=64)
            by_partition = words_in[which].rearrange("g p n t -> p g (n t)")
            if (which, c) == w_order[-1]:
                for i in range(RUN):
                    nc.sync.dma_start(
                        out=w_words[:, i, :].bitcast(I32), in_=by_partition[:, c * RUN + i, :].bitcast(I32)
                    )
            else:
                nc.sync.dma_start(out=w_words[:].bitcast(I32), in_=by_partition[:, group, :].bitcast(I32))
            w_tiles[(which, c)] = w_words

        def load_stream(n):
            if n + LEAD - 1 < CHUNKS:
                load_h(n + LEAD - 1)
            if n < len(w_order):
                load_w(*w_order[n])

        for which in ("q", "k"):
            nc.vector.memset(planes[which][:].bitcast(I32), 0)
        ident = keep.tile([P, P], F32)
        make_identity(nc, ident[:])
        for c in range(CHUNKS):
            load_scales("q", c)
        for c in range(LEAD):
            load_h(c)
        load_w(*w_order[0])
        for n in range(1, H_BUFS - LEAD + 1):
            load_stream(n)

        zero = keep.tile([P, 1], F32)
        one = keep.tile([P, 1], F32)
        nc.vector.memset(zero[:], 0.0)
        nc.scalar.activation(out=one[:], in_=zero[:], func=ACT.Exp)

        def out_of_psum(index, out_ap, in_ap):
            if index % 2 == 0:
                nc.scalar.copy(out=out_ap, in_=in_ap)
            else:
                nc.vector.tensor_copy(out=out_ap, in_=in_ap)

        def transpose_chunk(c):
            pairs = h_tiles[c][:].bitcast(F32)
            grouped = g_pool.tile([P, RUN, TOKENS, PACK], BF16, align_bytes=64)
            grouped_pairs = grouped[:].bitcast(F32)
            for i in range(RUN):
                flipped = psum.tile([P, 2, TOKENS], F32, name="flip%d" % i)
                for u in range(2):
                    for b in range(B):
                        nc.tensor.transpose(
                            flipped[:, u, b * NODES : (b + 1) * NODES],
                            pairs[:, b, 256 * i + u : 256 * (i + 1) : 2],
                            ident[:],
                        )
                out_of_psum(i, grouped_pairs[:, i], flipped[:].rearrange("p u r -> p r u"))
            return grouped

        def quantise_chunk(c, grouped):
            cols = slice(c * RUN * TOKENS, (c + 1) * RUN * TOKENS)
            nc.vector.quantize_mx(
                out=h_words[:, cols].bitcast(FP8X4),
                scales=h_planes[:, cols],
                in_=grouped[:].rearrange("p i r t -> p (i r t)"),
            )

        def project_chunk(which, c, acc):
            w_words = w_tiles[(which, c)]
            for i in range(RUN):
                g = c * RUN + i
                tokens = slice(g * TOKENS, (g + 1) * TOKENS)
                for j in range(D_BLOCKS):
                    features = slice(j * P, (j + 1) * P)
                    nc.tensor.matmul_mx(
                        out=acc[j][:],
                        lhsT=w_words[:, i, features].bitcast(FP8X4),
                        lhsT_scale=planes[which][LIVE * i : P, c, features],
                        rhs=h_words[:, tokens].bitcast(FP8X4),
                        rhs_scale=h_planes[:, tokens],
                        start=(g == 0),
                        stop=(g == PASSES - 1),
                    )

        def quantise_projection(which, acc, between=(None, None, None)):
            rounded = keep.tile([P, D_BLOCKS, TOKENS], BF16, name=which + "_rounded")
            for j in range(D_BLOCKS):
                out_of_psum(j, rounded[:, j, :], acc[j][:])
            grouped = keep.tile([P, TOKENS, PACK], BF16, name=which + "_grouped", align_bytes=64)
            codes = keep.tile([P, TOKENS], U32, name=which + "_codes", align_bytes=64)
            plane = keep.tile([P, TOKENS], U8, name=which + "_plane", align_bytes=64)
            halves = [slice(b * NODES, (b + 1) * NODES) for b in range(B)]
            nc.vector.tensor_copy(
                out=grouped[:, halves[0], :], in_=rounded[:, :, halves[0]].rearrange("p t r -> p r t")
            )
            nc.scalar.copy(
                out=grouped[:, halves[1], :], in_=rounded[:, :, halves[1]].rearrange("p t r -> p r t")
            )
            for b, nodes in enumerate(halves):
                if between[b] is not None:
                    between[b]()
                nc.vector.quantize_mx(
                    out=codes[:, nodes].bitcast(FP8X4),
                    scales=plane[:, nodes],
                    in_=grouped[:, nodes, :].rearrange("p r t -> p (r t)"),
                )
            if between[B] is not None:
                between[B]()
            return codes, plane


        q_acc = [psum.tile([P, TOKENS], F32, name="q_acc%d" % j) for j in range(D_BLOCKS)]
        for c in range(-LEAD, CHUNKS):
            if c >= 0:
                project_chunk("q", c, q_acc)
            if c + LEAD < CHUNKS:
                grouped = transpose_chunk(c + LEAD)
            load_stream(c + H_BUFS + 1)
            if c + LEAD < CHUNKS:
                quantise_chunk(c + LEAD, grouped)
        q_codes, q_plane = quantise_projection("q", q_acc)

        k_acc = [
            psum.tile([P, TOKENS], F32, name="k_acc%d" % j, tag="flip%d" % j) for j in range(D_BLOCKS)
        ]
        for c in range(CHUNKS):
            load_stream(CHUNKS + H_BUFS + 1 + c)
            project_chunk("k", c, k_acc)
        a_stat = keep.tile([P, NODES], BF16)
        m_mask = keep.tile([P, NODES], BF16)
        nc.sync.dma_start(out=a_stat[:], in_=A_stat)
        nc.sync.dma_start(out=m_mask[:], in_=M_mask)
        masked = keep.tile([P, NODES], F32)
        excluded = keep.tile([P, NODES], F32)
        bias = keep.tile([P, NODES], F32)
        bias_steps = (
            lambda: nc.vector.tensor_scalar(
                out=masked[:], in0=m_mask[:], scalar1=0.0, scalar2=None, op0=ALU.is_le
            ),
            lambda: nc.vector.tensor_tensor(out=excluded[:], in0=masked[:], in1=ident[:], op=ALU.max),
            lambda: nc.vector.scalar_tensor_tensor(
                out=bias[:], in0=excluded[:], scalar=EXCLUDED, in1=a_stat[:], op0=ALU.mult, op1=ALU.add
            ),
        )
        k_codes, k_plane = quantise_projection("k", k_acc, between=bias_steps)


        logits = psum.tile([P, B, NODES], F32, tag="q_acc0")
        for b in range(B):
            nodes = slice(b * NODES, (b + 1) * NODES)
            sides = ((q_codes, q_plane, k_codes, k_plane), (k_codes, k_plane, q_codes, q_plane))
            for turn, (l_codes, l_plane, r_codes, r_plane) in enumerate(sides):
                nc.tensor.matmul_mx(
                    out=logits[:, b, :],
                    lhsT=l_codes[:, nodes].bitcast(FP8X4),
                    lhsT_scale=l_plane[:, nodes],
                    rhs=r_codes[:, nodes].bitcast(FP8X4),
                    rhs_scale=r_plane[:, nodes],
                    start=(turn == 0),
                    stop=(turn == 1),
                )
        scores = keep.tile([P, B, NODES], F32)
        neg_max = keep.tile([P, B], F32)
        weights = keep.tile([P, B, NODES], F32)
        sums = keep.tile([P, B], F32)
        inverse = keep.tile([P, B], F32)
        result = keep.tile([P, B, NODES], F32)
        for b in range(B):
            nc.vector.scalar_tensor_tensor(
                out=scores[:, b, :], in0=logits[:, b, :], scalar=SCORE_SCALE, in1=bias[:],
                op0=ALU.mult, op1=ALU.add,
            )
        for b in range(B):
            nc.vector.tensor_reduce(
                out=neg_max[:, b : b + 1], in_=scores[:, b, :], axis=mybir.AxisListType.X,
                op=ALU.max, negate=True,
            )
            nc.scalar.activation(
                out=weights[:, b, :], in_=scores[:, b, :], func=ACT.Exp,
                bias=neg_max[:, b : b + 1], scale=1.0, accum_out=sums[:, b : b + 1],
            )
        for b in range(B):
            nc.vector.reciprocal(out=inverse[:, b : b + 1], in_=sums[:, b : b + 1])
            nc.vector.tensor_scalar(
                out=result[:, b, :], in0=weights[:, b, :], scalar1=inverse[:, b : b + 1],
                scalar2=None, op0=ALU.mult,
            )
        nc.sync.dma_start(out=out.rearrange("b n m -> n b m"), in_=result[:])
